import numpy as np
import ml_dtypes


def mxq(x, axis, fmt="e4m3"):
    dtype, down = {"e4m3": (ml_dtypes.float8_e4m3fn, 7), "e5m2": (ml_dtypes.float8_e5m2, 14)}[fmt]
    v = np.moveaxis(np.asarray(x, np.float32).astype(ml_dtypes.bfloat16).astype(np.float64), axis, -1)
    blocks = v.reshape(v.shape[:-1] + (-1, 32))
    amax = np.abs(blocks).max(-1, keepdims=True)
    byte = np.maximum(np.where(amax > 0, np.frexp(amax)[1] - 1 + 127, 0) - down, 1)
    scale = np.exp2(byte - 127.0)
    codes = (blocks / scale).astype(np.float32).astype(dtype).astype(np.float64)
    return np.moveaxis((codes * scale).reshape(v.shape), -1, axis)


WIDE = False


def mx_kscale(k):
    if not WIDE:
        return np.ones(k)
    levels = np.array([10, -10, 5, -5, 0])
    if k % 512:
        return np.exp2(np.random.permutation(np.resize(levels, k // 32))).repeat(32)
    a = np.empty((k // 512, 16))
    for p in range(k // 512):
        a[p, :8] = np.random.permutation(np.resize(levels, 8))
        for g in range(8):
            far = levels[np.abs(levels - a[p, g]) >= 10]
            a[p, g + 8] = far[np.random.randint(len(far))]
    return np.exp2(a.ravel()).repeat(32)


BF16 = ml_dtypes.bfloat16


def bf(x):
    return np.asarray(x, np.float32).astype(BF16)


def f64(x):
    return np.asarray(x).astype(np.float64)


B, T, C, HQ, HKV, HD = 4, 256, 2048, 16, 4, 128
EPS = 1e-6


def apply_rope(u, cos, sin):
    c = cos[None, :, None, :]
    s = sin[None, :, None, :]
    u1, u2 = u[..., ::2], u[..., 1::2]
    return np.concatenate([u1 * c - u2 * s, u1 * s + u2 * c], axis=-1)


def rmsnorm(u, w):
    return w * (u / np.sqrt(np.mean(u * u, axis=-1, keepdims=True) + EPS))


def draw0():
    s = mx_kscale(C)
    inv_freq = 1.0 / (10000.0 ** (np.arange(0, HD, 2) / HD))
    freqs = np.arange(T)[:, None] * inv_freq[None, :]
    return {"x": bf(np.random.standard_normal((B, T, C)) * s),
            "Wq": bf(np.random.standard_normal((HQ * HD, C)) / np.sqrt(C) / s),
            "bq": bf(np.random.standard_normal(HQ * HD) * 0.3),
            "Wk": bf(np.random.standard_normal((HKV * HD, C)) / np.sqrt(C) / s),
            "bk": bf(np.random.standard_normal(HKV * HD) * 0.3),
            "qn_w": bf(1.0 + 0.1 * np.random.standard_normal(HD)),
            "kn_w": bf(1.0 + 0.1 * np.random.standard_normal(HD)),
            "cos": bf(np.cos(freqs)),
            "sin": bf(np.sin(freqs))}


def core(x, Wq, bq, Wk, bk, qn_w, kn_w, cos, sin):
    xq = mxq(f64(x).reshape(B * T, C), 1, "e4m3")
    q = ((xq @ mxq(f64(Wq), 1, "e4m3").T) + f64(bq)).reshape(B, T, HQ, HD)
    k = ((xq @ mxq(f64(Wk), 1, "e4m3").T) + f64(bk)).reshape(B, T, HKV, HD)
    q = rmsnorm(apply_rope(q, f64(cos), f64(sin)), f64(qn_w))
    k = rmsnorm(apply_rope(k, f64(cos), f64(sin)), f64(kn_w))
    return q, k


def e4m3fn_bytes(y):
    return np.clip(np.asarray(y, np.float64), -448.0, 448.0).astype(np.float32).astype(ml_dtypes.float8_e4m3fn).view(np.uint8)


def e4m3fn_values(b):
    return np.asarray(b, np.uint8).view(ml_dtypes.float8_e4m3fn).astype(np.float64)


def setup_inputs():
    d = draw0()
    x0 = np.asarray(d['Wq']).astype(np.float64)
    s = (np.max(np.abs(x0), axis=(0,), keepdims=True) / 448.0).astype(np.float32)
    out = {}
    for k, v in d.items():
        if k == 'Wq':
            out['Wq_bytes'] = e4m3fn_bytes(x0 / s.astype(np.float64))
            out['Wq_scale'] = s
        else:
            out[k] = v
    return out


def reference(x, Wq_bytes, Wq_scale, bq, Wk, bk, qn_w, kn_w, cos, sin):
    return core(x, e4m3fn_values(Wq_bytes) * Wq_scale.astype(np.float64), bq, Wk, bk, qn_w, kn_w, cos, sin)

@@ -1,0 +1,411 @@
+from contextlib import ExitStack
+
+import concourse.mybir as mybir
+from concourse.masks import make_identity
+
+F32 = mybir.dt.float32
+BF16 = mybir.dt.bfloat16
+U32 = mybir.dt.uint32
+U8 = mybir.dt.uint8
+FP8 = mybir.dt.float8_e4m3fn
+FP8X4 = mybir.dt.float8_e4m3fn_x4
+ALU = mybir.AluOpType
+ACT = mybir.ActivationFunctionType
+
+P = 128
+K = 2048
+PASSES = 4
+TOKENS = 1024
+HALF = 512
+EPS = 1e-6
+N_Q_PAIRS = 8
+N_K_PAIRS = 2
+N_PAIRS = N_Q_PAIRS + N_K_PAIRS
+N_UNITS = 2 * N_PAIRS
+N_WARM = 6
+
+FLOPS = 2 * TOKENS * (2048 + 512) * K
+
+
+def tile_gqaselfattention_pa_kernel(
+    tc, x, Wq_bytes, Wq_scale, bq, Wk, bk, qn_w, kn_w, cos, sin, out_0, out_1
+):
+    nc = tc.nc
+    x_view = x.flatten_outer_dims().rearrange("(n p) k -> n p k", p=P)
+    wq_view = Wq_bytes.rearrange("(j p e) k -> j p e k", p=P, e=2)
+    wk_view = Wk.rearrange("(j p e) k -> j p e k", p=P, e=2)
+    oq_view = out_0.rearrange("b t h d -> (b t) (h d)").rearrange("(n p) c -> p n c", p=P)
+    ok_view = out_1.rearrange("b t h d -> (b t) (h d)").rearrange("(n p) c -> p n c", p=P)
+    order = [N_Q_PAIRS, N_Q_PAIRS + 1] + list(range(N_Q_PAIRS))
+
+    with ExitStack() as ctx:
+        const = ctx.enter_context(tc.tile_pool(name="const", bufs=1))
+        xin = ctx.enter_context(tc.tile_pool(name="xin", bufs=8))
+        xkeep = ctx.enter_context(tc.tile_pool(name="xkeep", bufs=1))
+        bpool = ctx.enter_context(tc.tile_pool(name="bpool", bufs=3))
+        wpool = ctx.enter_context(tc.tile_pool(name="wpool", bufs=3))
+        gpool = ctx.enter_context(tc.tile_pool(name="gpool", bufs=2))
+        tpool = ctx.enter_context(tc.tile_pool(name="tpool", bufs=2))
+        ypool = ctx.enter_context(tc.tile_pool(name="ypool", bufs=3))
+        spool = ctx.enter_context(tc.tile_pool(name="spool", bufs=4))
+        ps_tp = ctx.enter_context(tc.psum_pool(name="ps_tp", bufs=2))
+        ps_mx = ctx.enter_context(tc.psum_pool(name="ps_mx", bufs=4))
+        ps_ot = ctx.enter_context(tc.psum_pool(name="ps_ot", bufs=2))
+
+        cs_bf = const.tile([P, 2, 2, 64], BF16, name="cs_bf")
+        brow_bf = const.tile([P, 256], BF16, name="brow_bf")
+        warm = const.tile([P, 1], F32, name="warm")
+        warm_out = const.tile([P, 1], F32, name="warm_out")
+        ident = const.tile([P, P], F32, name="ident")
+        sc_bc = const.tile([P, K], F32, name="sc_bc")
+        wq_bc = const.tile([P, P], BF16, name="wq_bc")
+        wk_bc = const.tile([P, P], BF16, name="wk_bc")
+        zeros = const.tile([P, HALF], BF16, name="zeros")
+        nc.vector.memset(zeros[:], 0.0)
+        nc.vector.memset(brow_bf[:], 0.0)
+        nc.vector.memset(warm[:], 1.0)
+        make_identity(nc, ident[:])
+
+        x_sb = []
+        for n in range(8):
+            xt = xin.tile([P, K], BF16, name="x_sb", tag="x_sb")
+            x_sb.append(xt)
+        xc = xkeep.tile([P, PASSES, TOKENS], U32, name="xc", align_bytes=64)
+        xs = xkeep.tile([P, PASSES, TOKENS], U8, name="xs", align_bytes=64)
+        xg = []
+        for h in range(2):
+            xgh = xkeep.tile([P, PASSES, HALF, 4], BF16, name="xg%d" % h, align_bytes=64)
+            xg.append(xgh)
+
+        ctx.enter_context(tc.manual_schedule())
+
+        nc.scalar.dma_start(out=cs_bf[:, 0, :, :], in_=cos.rearrange("(b p) i -> p b i", p=P))
+        nc.scalar.dma_start(out=cs_bf[:, 1, :, :], in_=sin.rearrange("(b p) i -> p b i", p=P))
+        nc.scalar.dma_start(out=brow_bf[0:N_Q_PAIRS, :], in_=bq.rearrange("(j c) -> j c", c=256))
+        nc.scalar.dma_start(
+            out=brow_bf[N_Q_PAIRS : N_Q_PAIRS + N_K_PAIRS, :], in_=bk.rearrange("(j c) -> j c", c=256)
+        )
+        nc.scalar.activation(out=warm_out[:], in_=warm[:], func=ACT.Abs_reciprocal_sqrt)
+
+        wb_of = {}
+        by_of = {}
+        wg_of = {}
+        codes_of = {}
+        acc_of = {}
+        prods_of = {}
+        ots_of = {}
+        rstd_of = {}
+        late = []
+
+        def load_x(i):
+            nc.sync.dma_start(out=x_sb[i][:], in_=x_view[i])
+
+        def load_w(n):
+            j = order[n]
+            if j >= N_Q_PAIRS:
+                wb = wpool.tile([P, 2, K], BF16, name="wb", tag="wb")
+                wb_of[n] = wb
+                nc.sync.dma_start(out=wb[:], in_=wk_view[j - N_Q_PAIRS])
+            else:
+                by = bpool.tile([P, 2, K], U8, name="wq_bytes_sb", tag="wq_bytes_sb")
+                by_of[n] = by
+                nc.sync.dma_start(out=by[:], in_=wq_view[j])
+
+        def prod(n, e):
+            if order[n] >= N_Q_PAIRS:
+                return
+            if e == 0:
+                wb = wpool.tile([P, 2, K], BF16, name="wb", tag="wb")
+                wb_of[n] = wb
+            nc.vector.tensor_tensor(
+                out=wb_of[n][:, e, :], in0=by_of[n][:, e, :].bitcast(FP8), in1=sc_bc[:], op=ALU.mult
+            )
+
+        def flush_late():
+            for tp, dst in late:
+                nc.scalar.copy(out=dst, in_=tp[:].rearrange("p g u r -> p g r u"))
+            late.clear()
+
+        def dummy(bank):
+            nc.tensor.matmul(
+                out=bank[:].rearrange("p a b c -> p (a b c)"), lhsT=zeros[:, 0:P], rhs=zeros[:], start=True, stop=True
+            )
+
+        def head_bank(where):
+            if where == "mx":
+                bank = ps_mx.tile([P, 2, 2, P], F32, name="mx", tag="mx")
+            elif where == "ot":
+                bank = ps_ot.tile([P, 2, 2, P], F32, name="ot", tag="ot")
+            else:
+                bank = ps_tp.tile([P, 2, 2, P], F32, name="tp", tag="tp")
+            return bank
+
+        def transpose_rows(src_bf, dst_words, defer, where=("tp", "tp"), warm_first=False):
+            words = src_bf.bitcast(F32)
+            for gp in range(2):
+                tp = head_bank(where[gp])
+                if warm_first and gp == 0:
+                    dummy(tp)
+                for g2 in range(2):
+                    g = 2 * gp + g2
+                    for u in range(2):
+                        nc.tensor.transpose(
+                            tp[:, g2, u, :], words[:, 256 * g + u : 256 * (g + 1) : 2], ident[:]
+                        )
+                late.append((tp, dst_words[:, 2 * gp : 2 * gp + 2, :, :]))
+                if not (defer and gp == 1):
+                    flush_late()
+
+        def xt_(i):
+            h, tl = divmod(i, 4)
+            transpose_rows(
+                x_sb[i][:], xg[h][:].bitcast(F32)[:, :, tl * P : (tl + 1) * P, :], False,
+                ("mx", "mx") if h == 0 else ("tp", "ot"), True,
+            )
+
+        def qx(h, tp2):
+            for g in range(PASSES):
+                lo = h * HALF + tp2 * 256
+                nc.vector.quantize_mx(
+                    out=xc[:, g, lo : lo + 256].bitcast(FP8X4),
+                    scales=xs[:, g, lo : lo + 256],
+                    in_=xg[h][:, g, tp2 * 256 : (tp2 + 1) * 256, :].rearrange("p n t -> p (n t)"),
+                )
+
+        def bt(n, e, defer, where=("tp", "tp"), warm_first=False):
+            if e == 0:
+                wg = gpool.tile([P, 2, PASSES, P, 4], BF16, name="wg", tag="wg", align_bytes=64)
+                wg_of[n] = wg
+            transpose_rows(wb_of[n][:, e, :], wg_of[n][:].bitcast(F32)[:, e, :, :, :], defer, where, warm_first)
+
+        def qw(n):
+            wc = wpool.tile([P, 2 * PASSES * P], U32, name="wc", tag="wc", align_bytes=64)
+            ws = wpool.tile([P, 2 * PASSES * P], U8, name="ws", tag="ws", align_bytes=64)
+            nc.vector.quantize_mx(
+                out=wc[:].bitcast(FP8X4), scales=ws[:], in_=wg_of[n][:].rearrange("p e g r t -> p (e g r t)")
+            )
+            codes_of[n] = (wc, ws)
+
+        cs_f = const.tile([P, 2, 2, 2, 64], F32, name="cs_f")
+        brow_f = const.tile([P, 256], F32, name="brow_f")
+
+        def setup_widen():
+            for hh in range(2):
+                nc.vector.tensor_copy(out=cs_f[:, :, :, hh, :], in_=cs_bf[:])
+            nc.vector.tensor_copy(out=brow_f[:], in_=brow_bf[:])
+
+        def setup_tables():
+            tp_cs = ps_ot.tile([P, 2, 2, P], F32, name="ot", tag="ot")
+            for c in range(2):
+                for b in range(2):
+                    nc.tensor.transpose(
+                        tp_cs[:, c, b, :], cs_f[:, c, b, :, :].rearrange("p h i -> p (h i)"), ident[:]
+                    )
+            for rep in range(2):
+                nc.vector.tensor_copy(out=ctab[:, rep, :], in_=tp_cs[:, 0, :, :].rearrange("p b t -> p (b t)"))
+                nc.vector.tensor_copy(out=stab[:, rep, :], in_=tp_cs[:, 1, :, :].rearrange("p b t -> p (b t)"))
+                nc.vector.tensor_scalar_mul(
+                    out=ntab[:, rep, :], in0=tp_cs[:, 1, :, :].rearrange("p b t -> p (b t)"), scalar1=-1.0
+                )
+            tp_b = ps_ot.tile([P, 2, 2, P], F32, name="ot", tag="ot")
+            brow_v = brow_f[:].rearrange("p (c e) -> p e c", e=2)
+            for e in range(2):
+                nc.tensor.transpose(tp_b[:, 0, e, :], brow_v[:, e, :], ident[:])
+            nc.vector.tensor_copy(out=bias_sb[:, :, 0:10], in_=tp_b[:, 0, :, 0:10])
+
+        def setup_gains():
+            for wr, src in ((w_rep_q, wq_bc), (w_rep_k, wk_bc)):
+                for r in range(4):
+                    nc.gpsimd.tensor_copy(out=wr[:, r, :], in_=src[:])
+
+        ctab = const.tile([P, 2, 256], F32, name="ctab")
+        stab = const.tile([P, 2, 256], F32, name="stab")
+        ntab = const.tile([P, 2, 256], F32, name="ntab")
+        bias_sb = const.tile([P, 2, 16], F32, name="bias_sb")
+        w_rep_q = const.tile([P, 4, P], F32, name="w_rep_q")
+        w_rep_k = const.tile([P, 4, P], F32, name="w_rep_k")
+        ctab_f = ctab[:].rearrange("p r t -> p (r t)")
+        stab_f = stab[:].rearrange("p r t -> p (r t)")
+        ntab_f = ntab[:].rearrange("p r t -> p (r t)")
+
+        def mx(u):
+            n, h = divmod(u, 2)
+            wc, ws = codes_of[n]
+            tok = slice(h * HALF, (h + 1) * HALF)
+            acc = []
+            for e in range(2):
+                pe = ps_mx.tile([P, HALF], F32, name="mx", tag="mx")
+                acc.append(pe)
+                for g in range(PASSES):
+                    c = e * PASSES + g
+                    nc.tensor.matmul_mx(
+                        out=pe[:],
+                        lhsT=wc[:, c * P : (c + 1) * P].bitcast(FP8X4),
+                        lhsT_scale=ws[:, c * P : (c + 1) * P],
+                        rhs=xc[:, g, tok].bitcast(FP8X4),
+                        rhs_scale=xs[:, g, tok],
+                        start=(g == 0),
+                        stop=(g == PASSES - 1),
+                    )
+            acc_of[u] = acc
+
+        def rp(u):
+            j = order[u // 2]
+            acc = acc_of[u]
+            prods = []
+            for i, (e, tab) in enumerate(((0, ctab_f), (1, ntab_f), (0, stab_f), (1, ctab_f))):
+                t = tpool.tile([P, HALF], F32, name="t%d" % i, tag="t%d" % i)
+                nc.vector.scalar_tensor_tensor(
+                    out=t[:], in0=acc[e][:], scalar=bias_sb[:, e, j : j + 1], in1=tab, op0=ALU.add, op1=ALU.mult
+                )
+                prods.append(t)
+            prods_of[u] = prods
+
+        def ot_sq(u):
+            prods = prods_of[u]
+            ss = spool.tile([P, 8], F32, name="ss", tag="ss")
+            ots = []
+            for b2 in range(2):
+                ot = ps_ot.tile([P, 2, 2, P], F32, name="ot", tag="ot")
+                ots.append(ot)
+                for bb in range(2):
+                    cols = slice((2 * b2 + bb) * P, (2 * b2 + bb + 1) * P)
+                    for half in range(2):
+                        nc.tensor.matmul(
+                            out=ot[:, bb, half, :], lhsT=prods[2 * half][:, cols], rhs=ident[:],
+                            start=True, stop=False, is_transpose=True,
+                        )
+                        nc.tensor.matmul(
+                            out=ot[:, bb, half, :], lhsT=prods[2 * half + 1][:, cols], rhs=ident[:],
+                            start=False, stop=True, is_transpose=True,
+                        )
+            for b2 in range(2):
+                for bb in range(2):
+                    for hh in range(2):
+                        col = (2 * b2 + bb) * 2 + hh
+                        junk = spool.tile([P, 2, 64], F32, name="junk", tag="junk")
+                        nc.scalar.activation(
+                            out=junk[:], in_=ots[b2][:, bb, :, hh * 64 : (hh + 1) * 64], func=ACT.Square,
+                            accum_out=ss[:, col : col + 1],
+                        )
+            rstd = spool.tile([P, 8], F32, name="rstd", tag="rstd")
+            nc.scalar.activation(
+                out=rstd[:], in_=ss[:], func=ACT.Abs_reciprocal_sqrt, bias=EPS, scale=1.0 / 128.0
+            )
+            ots_of[u] = ots
+            rstd_of[u] = rstd
+
+        def finish(u, on_vector):
+            n, h = divmod(u, 2)
+            j = order[n]
+            ots = ots_of[u]
+            rstd = rstd_of[u]
+            wr = w_rep_q if j < N_Q_PAIRS else w_rep_k
+            if j < N_Q_PAIRS:
+                dst = oq_view[:, 4 * h : 4 * h + 4, 256 * j : 256 * (j + 1)]
+            else:
+                dst = ok_view[:, 4 * h : 4 * h + 4, 256 * (j - N_Q_PAIRS) : 256 * (j - N_Q_PAIRS + 1)]
+            y = ypool.tile([P, 4, 2, P], F32, name="y", tag="y")
+            yf = y[:].rearrange("p b h d -> p (b h d)")
+            for b2 in range(2):
+                for bb in range(2):
+                    for hh in range(2):
+                        blk = 2 * b2 + bb
+                        col = blk * 2 + hh
+                        if on_vector:
+                            nc.vector.scalar_tensor_tensor(
+                                out=y[:, blk, hh, :].rearrange("p (a i) -> p a i", a=2),
+                                in0=ots[b2][:, bb, :, hh * 64 : (hh + 1) * 64],
+                                scalar=rstd[:, col : col + 1],
+                                in1=wr[:, 0, :].rearrange("p (a i) -> p a i", a=2),
+                                op0=ALU.mult,
+                                op1=ALU.mult,
+                            )
+                        else:
+                            nc.scalar.activation(
+                                out=y[:, blk, hh, :].rearrange("p (a i) -> p a i", a=2),
+                                in_=ots[b2][:, bb, :, hh * 64 : (hh + 1) * 64],
+                                func=ACT.Copy,
+                                scale=rstd[:, col : col + 1],
+                            )
+                if not on_vector:
+                    nc.gpsimd.tensor_tensor(
+                        out=yf[:, b2 * 512 : (b2 + 1) * 512],
+                        in0=yf[:, b2 * 512 : (b2 + 1) * 512],
+                        in1=wr[:].rearrange("p r d -> p (r d)"),
+                        op=ALU.mult,
+                    )
+                nc.sync.dma_start(
+                    out=dst[:, 2 * b2 : 2 * b2 + 2, :],
+                    in_=y[:, 2 * b2 : 2 * b2 + 2, :, :].rearrange("p b h d -> p b (h d)"),
+                )
+
+        for i in range(4):
+            load_x(i)
+        load_w(0)
+        nc.sync.dma_start(out=sc_bc[:], in_=Wq_scale.rearrange("o k -> (o k)").partition_broadcast(P))
+        load_w(2)
+        for i in range(4, 8):
+            load_x(i)
+        load_w(1)
+        load_w(3)
+        nc.sync.dma_start(out=wq_bc[:], in_=qn_w.partition_broadcast(P))
+        nc.sync.dma_start(out=wk_bc[:], in_=kn_w.partition_broadcast(P))
+        load_w(4)
+
+        setup_widen()
+        first = head_bank("mx")
+        for i in range(N_WARM):
+            dummy(first)
+        xt_(0)
+        xt_(1)
+        qx(0, 0)
+        xt_(2)
+        xt_(3)
+        qx(0, 1)
+        setup_tables()
+        bt(0, 0, False, ("mx", "mx"), True)
+        bt(0, 1, False, ("mx", "mx"), True)
+        qw(0)
+        prod(2, 0)
+
+        mx(0)
+        prod(2, 1)
+        xt_(4)
+        xt_(5)
+        rp(0)
+        qx(1, 0)
+        xt_(6)
+        xt_(7)
+        setup_gains()
+        qx(1, 1)
+        bt(1, 0, False, ("tp", "ot"), True)
+        bt(1, 1, False, ("tp", "ot"), True)
+        qw(1)
+
+        ot_sq(0)
+        mx(1)
+        prod(3, 0)
+        bt(2, 0, False)
+        rp(1)
+
+        for k in range(1, N_UNITS):
+            if k + 1 < N_UNITS:
+                mx(k + 1)
+            n, e = divmod(k + 6, 2)
+            if n < N_PAIRS:
+                prod(n, e)
+            if e == 1 and n + 2 < N_PAIRS:
+                load_w(n + 2)
+            finish(k - 1, False)
+            n, e = divmod(k + 4, 2)
+            if n < N_PAIRS:
+                bt(n, e, True)
+            if k + 1 < N_UNITS:
+                rp(k + 1)
+            ot_sq(k)
+            flush_late()
+            n, e = divmod(k + 3, 2)
+            if e == 0 and n < N_PAIRS:
+                qw(n)
+        finish(N_UNITS - 1, True)

@@ -23,6 +23,7 @@ N_K_PAIRS = 2
 N_PAIRS = N_Q_PAIRS + N_K_PAIRS
 N_UNITS = 2 * N_PAIRS
 N_WARM = 6
+V_TAIL = 2
 
 FLOPS = 2 * TOKENS * (2048 + 512) * K
 
@@ -36,13 +37,14 @@ def tile_gqaselfattention_pa_kernel(
     wk_view = Wk.rearrange("(j p e) k -> j p e k", p=P, e=2)
     oq_view = out_0.rearrange("b t h d -> (b t) (h d)").rearrange("(n p) c -> p n c", p=P)
     ok_view = out_1.rearrange("b t h d -> (b t) (h d)").rearrange("(n p) c -> p n c", p=P)
-    order = [N_Q_PAIRS, N_Q_PAIRS + 1] + list(range(N_Q_PAIRS))
+    order = [0, 1, 8, 2, 3, 4, 9, 5, 6, 7]
 
     with ExitStack() as ctx:
         const = ctx.enter_context(tc.tile_pool(name="const", bufs=1))
         xin = ctx.enter_context(tc.tile_pool(name="xin", bufs=8))
         xkeep = ctx.enter_context(tc.tile_pool(name="xkeep", bufs=1))
-        bpool = ctx.enter_context(tc.tile_pool(name="bpool", bufs=3))
+        bpool = ctx.enter_context(tc.tile_pool(name="bpool", bufs=4))
+        wbpool = ctx.enter_context(tc.tile_pool(name="wbpool", bufs=5))
         wpool = ctx.enter_context(tc.tile_pool(name="wpool", bufs=3))
         gpool = ctx.enter_context(tc.tile_pool(name="gpool", bufs=2))
         tpool = ctx.enter_context(tc.tile_pool(name="tpool", bufs=2))
@@ -94,7 +96,9 @@ def tile_gqaselfattention_pa_kernel(
         acc_of = {}
         prods_of = {}
         ots_of = {}
+        ss_of = {}
         rstd_of = {}
+        y_of = {}
         late = []
 
         def load_x(i):
@@ -103,7 +107,7 @@ def tile_gqaselfattention_pa_kernel(
         def load_w(n):
             j = order[n]
             if j >= N_Q_PAIRS:
-                wb = wpool.tile([P, 2, K], BF16, name="wb", tag="wb")
+                wb = wbpool.tile([P, 2, K], BF16, name="wb", tag="wb")
                 wb_of[n] = wb
                 nc.sync.dma_start(out=wb[:], in_=wk_view[j - N_Q_PAIRS])
             else:
@@ -112,10 +116,8 @@ def tile_gqaselfattention_pa_kernel(
                 nc.sync.dma_start(out=by[:], in_=wq_view[j])
 
         def prod(n, e):
-            if order[n] >= N_Q_PAIRS:
-                return
             if e == 0:
-                wb = wpool.tile([P, 2, K], BF16, name="wb", tag="wb")
+                wb = wbpool.tile([P, 2, K], BF16, name="wb", tag="wb")
                 wb_of[n] = wb
             nc.vector.tensor_tensor(
                 out=wb_of[n][:, e, :], in0=by_of[n][:, e, :].bitcast(FP8), in1=sc_bc[:], op=ALU.mult
@@ -156,12 +158,9 @@ def tile_gqaselfattention_pa_kernel(
                 if not (defer and gp == 1):
                     flush_late()
 
-        def xt_(i):
+        def xt_(i, where):
             h, tl = divmod(i, 4)
-            transpose_rows(
-                x_sb[i][:], xg[h][:].bitcast(F32)[:, :, tl * P : (tl + 1) * P, :], False,
-                ("mx", "mx") if h == 0 else ("tp", "ot"), True,
-            )
+            transpose_rows(x_sb[i][:], xg[h][:].bitcast(F32)[:, :, tl * P : (tl + 1) * P, :], False, where, True)
 
         def qx(h, tp2):
             for g in range(PASSES):
@@ -172,7 +171,8 @@ def tile_gqaselfattention_pa_kernel(
                     in_=xg[h][:, g, tp2 * 256 : (tp2 + 1) * 256, :].rearrange("p n t -> p (n t)"),
                 )
 
-        def bt(n, e, defer, where=("tp", "tp"), warm_first=False):
+        def bt(m, defer, where=("tp", "tp"), warm_first=False):
+            n, e = divmod(m, 2)
             if e == 0:
                 wg = gpool.tile([P, 2, PASSES, P, 4], BF16, name="wg", tag="wg", align_bytes=64)
                 wg_of[n] = wg
@@ -249,163 +249,211 @@ def tile_gqaselfattention_pa_kernel(
                     )
             acc_of[u] = acc
 
-        def rp(u):
+        def rp(u, pieces=1):
             j = order[u // 2]
             acc = acc_of[u]
             prods = []
-            for i, (e, tab) in enumerate(((0, ctab_f), (1, ntab_f), (0, stab_f), (1, ctab_f))):
+            for i in range(4):
                 t = tpool.tile([P, HALF], F32, name="t%d" % i, tag="t%d" % i)
-                nc.vector.scalar_tensor_tensor(
-                    out=t[:], in0=acc[e][:], scalar=bias_sb[:, e, j : j + 1], in1=tab, op0=ALU.add, op1=ALU.mult
-                )
                 prods.append(t)
+            width = HALF // pieces
+            for c in range(pieces):
+                cols = slice(c * width, (c + 1) * width)
+                for i, (e, tab) in enumerate(((0, ctab_f), (1, ntab_f), (0, stab_f), (1, ctab_f))):
+                    nc.vector.scalar_tensor_tensor(
+                        out=prods[i][:, cols], in0=acc[e][:, cols], scalar=bias_sb[:, e, j : j + 1], in1=tab[:, cols],
+                        op0=ALU.add, op1=ALU.mult,
+                    )
             prods_of[u] = prods
 
-        def ot_sq(u):
+        def ot(u, b2, where="ot"):
             prods = prods_of[u]
-            ss = spool.tile([P, 8], F32, name="ss", tag="ss")
-            ots = []
-            for b2 in range(2):
-                ot = ps_ot.tile([P, 2, 2, P], F32, name="ot", tag="ot")
-                ots.append(ot)
-                for bb in range(2):
-                    cols = slice((2 * b2 + bb) * P, (2 * b2 + bb + 1) * P)
-                    for half in range(2):
-                        nc.tensor.matmul(
-                            out=ot[:, bb, half, :], lhsT=prods[2 * half][:, cols], rhs=ident[:],
-                            start=True, stop=False, is_transpose=True,
-                        )
-                        nc.tensor.matmul(
-                            out=ot[:, bb, half, :], lhsT=prods[2 * half + 1][:, cols], rhs=ident[:],
-                            start=False, stop=True, is_transpose=True,
-                        )
-            for b2 in range(2):
-                for bb in range(2):
-                    for hh in range(2):
-                        col = (2 * b2 + bb) * 2 + hh
-                        junk = spool.tile([P, 2, 64], F32, name="junk", tag="junk")
-                        nc.scalar.activation(
-                            out=junk[:], in_=ots[b2][:, bb, :, hh * 64 : (hh + 1) * 64], func=ACT.Square,
-                            accum_out=ss[:, col : col + 1],
-                        )
-            rstd = spool.tile([P, 8], F32, name="rstd", tag="rstd")
-            nc.scalar.activation(
-                out=rstd[:], in_=ss[:], func=ACT.Abs_reciprocal_sqrt, bias=EPS, scale=1.0 / 128.0
-            )
-            ots_of[u] = ots
-            rstd_of[u] = rstd
+            bank = head_bank(where)
+            ots_of.setdefault(u, []).append(bank)
+            for bb in range(2):
+                cols = slice((2 * b2 + bb) * P, (2 * b2 + bb + 1) * P)
+                for half in range(2):
+                    nc.tensor.matmul(
+                        out=bank[:, bb, half, :], lhsT=prods[2 * half][:, cols], rhs=ident[:],
+                        start=True, stop=False, is_transpose=True,
+                    )
+                    nc.tensor.matmul(
+                        out=bank[:, bb, half, :], lhsT=prods[2 * half + 1][:, cols], rhs=ident[:],
+                        start=False, stop=True, is_transpose=True,
+                    )
 
-        def finish(u, on_vector):
+        def sq(u, b2):
+            if b2 == 0:
+                ss = spool.tile([P, 16], F32, name="ss", tag="ss")
+                ss_of[u] = ss
+                rstd = spool.tile([P, 16], F32, name="rstd", tag="rstd")
+                rstd_of[u] = rstd
+            for bb in range(2):
+                for hh in range(2):
+                    col = 8 * b2 + 2 * bb + hh
+                    junk = spool.tile([P, 2, 64], F32, name="junk", tag="junk")
+                    nc.scalar.activation(
+                        out=junk[:], in_=ots_of[u][b2][:, bb, :, hh * 64 : (hh + 1) * 64], func=ACT.Square,
+                        accum_out=ss_of[u][:, col : col + 1],
+                    )
+
+        def rs(u, b2):
+            nc.scalar.activation(
+                out=rstd_of[u][:, 8 * b2 : 8 * b2 + 4], in_=ss_of[u][:, 8 * b2 : 8 * b2 + 4],
+                func=ACT.Abs_reciprocal_sqrt, bias=EPS, scale=1.0 / 128.0,
+            )
+
+        def ot_sq(u):
+            ot(u, 0)
+            ot(u, 1)
+            sq(u, 0)
+            rs(u, 0)
+            sq(u, 1)
+            rs(u, 1)
+
+        def finish(u, b2, on_vector):
             n, h = divmod(u, 2)
             j = order[n]
-            ots = ots_of[u]
+            bank = ots_of[u][b2]
             rstd = rstd_of[u]
             wr = w_rep_q if j < N_Q_PAIRS else w_rep_k
             if j < N_Q_PAIRS:
                 dst = oq_view[:, 4 * h : 4 * h + 4, 256 * j : 256 * (j + 1)]
             else:
                 dst = ok_view[:, 4 * h : 4 * h + 4, 256 * (j - N_Q_PAIRS) : 256 * (j - N_Q_PAIRS + 1)]
-            y = ypool.tile([P, 4, 2, P], F32, name="y", tag="y")
+            if b2 == 0:
+                y = ypool.tile([P, 4, 2, P], F32, name="y", tag="y")
+                y_of[u] = y
+            y = y_of[u]
             yf = y[:].rearrange("p b h d -> p (b h d)")
-            for b2 in range(2):
-                for bb in range(2):
-                    for hh in range(2):
-                        blk = 2 * b2 + bb
-                        col = blk * 2 + hh
-                        if on_vector:
-                            nc.vector.scalar_tensor_tensor(
-                                out=y[:, blk, hh, :].rearrange("p (a i) -> p a i", a=2),
-                                in0=ots[b2][:, bb, :, hh * 64 : (hh + 1) * 64],
-                                scalar=rstd[:, col : col + 1],
-                                in1=wr[:, 0, :].rearrange("p (a i) -> p a i", a=2),
-                                op0=ALU.mult,
-                                op1=ALU.mult,
-                            )
-                        else:
-                            nc.scalar.activation(
-                                out=y[:, blk, hh, :].rearrange("p (a i) -> p a i", a=2),
-                                in_=ots[b2][:, bb, :, hh * 64 : (hh + 1) * 64],
-                                func=ACT.Copy,
-                                scale=rstd[:, col : col + 1],
-                            )
-                if not on_vector:
-                    nc.gpsimd.tensor_tensor(
-                        out=yf[:, b2 * 512 : (b2 + 1) * 512],
-                        in0=yf[:, b2 * 512 : (b2 + 1) * 512],
-                        in1=wr[:].rearrange("p r d -> p (r d)"),
-                        op=ALU.mult,
-                    )
-                nc.sync.dma_start(
-                    out=dst[:, 2 * b2 : 2 * b2 + 2, :],
-                    in_=y[:, 2 * b2 : 2 * b2 + 2, :, :].rearrange("p b h d -> p b (h d)"),
+            for bb in range(2):
+                for hh in range(2):
+                    blk = 2 * b2 + bb
+                    col = 8 * b2 + 2 * bb + hh
+                    if on_vector:
+                        nc.vector.scalar_tensor_tensor(
+                            out=y[:, blk, hh, :].rearrange("p (a i) -> p a i", a=2),
+                            in0=bank[:, bb, :, hh * 64 : (hh + 1) * 64],
+                            scalar=rstd[:, col : col + 1],
+                            in1=wr[:, 0, :].rearrange("p (a i) -> p a i", a=2),
+                            op0=ALU.mult,
+                            op1=ALU.mult,
+                        )
+                    else:
+                        nc.scalar.activation(
+                            out=y[:, blk, hh, :].rearrange("p (a i) -> p a i", a=2),
+                            in_=bank[:, bb, :, hh * 64 : (hh + 1) * 64],
+                            func=ACT.Copy,
+                            scale=rstd[:, col : col + 1],
+                        )
+            if not on_vector:
+                nc.gpsimd.tensor_tensor(
+                    out=yf[:, b2 * 512 : (b2 + 1) * 512],
+                    in0=yf[:, b2 * 512 : (b2 + 1) * 512],
+                    in1=wr[:].rearrange("p r d -> p (r d)"),
+                    op=ALU.mult,
                 )
+            nc.sync.dma_start(
+                out=dst[:, 2 * b2 : 2 * b2 + 2, :],
+                in_=y[:, 2 * b2 : 2 * b2 + 2, :, :].rearrange("p b h d -> p b (h d)"),
+            )
 
-        for i in range(4):
-            load_x(i)
-        load_w(0)
         nc.sync.dma_start(out=sc_bc[:], in_=Wq_scale.rearrange("o k -> (o k)").partition_broadcast(P))
-        load_w(2)
-        for i in range(4, 8):
-            load_x(i)
-        load_w(1)
-        load_w(3)
+        for kind, i in (("w", 0), ("x", 0), ("x", 1), ("x", 2), ("x", 3), ("w", 1), ("x", 4), ("x", 5), ("x", 6), ("x", 7), ("w", 2), ("w", 3), ("w", 4)):
+            if kind == "x":
+                load_x(i)
+            else:
+                load_w(i)
         nc.sync.dma_start(out=wq_bc[:], in_=qn_w.partition_broadcast(P))
         nc.sync.dma_start(out=wk_bc[:], in_=kn_w.partition_broadcast(P))
-        load_w(4)
+        state = {"p": 0, "l": 5}
+        qhalves = [2 * n + e for n in range(N_PAIRS) for e in range(2) if order[n] < N_Q_PAIRS]
+
+        def more_loads():
+            if state["l"] < N_PAIRS:
+                load_w(state["l"])
+                state["l"] += 1
+
+        def next_prod(c=1):
+            for i in range(c):
+                if state["p"] < len(qhalves):
+                    n, e = divmod(qhalves[state["p"]], 2)
+                    prod(n, e)
+                    state["p"] += 1
+                    if e == 1:
+                        more_loads()
+
+        def due(k):
+            return state["p"] < len(qhalves) and qhalves[state["p"]] <= k + 5
 
         setup_widen()
         first = head_bank("mx")
         for i in range(N_WARM):
             dummy(first)
-        xt_(0)
-        xt_(1)
-        qx(0, 0)
-        xt_(2)
-        xt_(3)
-        qx(0, 1)
         setup_tables()
-        bt(0, 0, False, ("mx", "mx"), True)
-        bt(0, 1, False, ("mx", "mx"), True)
+        next_prod(2)
+        xt_(0, ("mx", "mx"))
+        xt_(1, ("mx", "mx"))
+        qx(0, 0)
+        bt(0, False, ("mx", "mx"))
+        xt_(2, ("mx", "mx"))
+        bt(1, False, ("mx", "mx"))
+        xt_(3, ("mx", "mx"))
+        next_prod(1)
+        qx(0, 1)
         qw(0)
-        prod(2, 0)
-
+        xt_(4, ("tp", "ot"))
+        xt_(5, ("tp", "ot"))
         mx(0)
-        prod(2, 1)
-        xt_(4)
-        xt_(5)
-        rp(0)
         qx(1, 0)
-        xt_(6)
-        xt_(7)
-        setup_gains()
+        xt_(6, ("tp", "ot"))
+        xt_(7, ("tp", "ot"))
+        next_prod(1)
         qx(1, 1)
-        bt(1, 0, False, ("tp", "ot"), True)
-        bt(1, 1, False, ("tp", "ot"), True)
-        qw(1)
-
-        ot_sq(0)
+        rp(0)
         mx(1)
-        prod(3, 0)
-        bt(2, 0, False)
+        bt(2, False, ("tp", "ot"))
+        bt(3, False, ("tp", "ot"))
+        setup_gains()
+        next_prod(1)
+        qw(1)
         rp(1)
+        ot_sq(0)
+        bt(4, False)
 
         for k in range(1, N_UNITS):
+            by_vector = k - 1 >= N_UNITS - V_TAIL
             if k + 1 < N_UNITS:
                 mx(k + 1)
-            n, e = divmod(k + 6, 2)
-            if n < N_PAIRS:
-                prod(n, e)
-            if e == 1 and n + 2 < N_PAIRS:
-                load_w(n + 2)
-            finish(k - 1, False)
-            n, e = divmod(k + 4, 2)
-            if n < N_PAIRS:
-                bt(n, e, True)
+            if due(k) or k % 2 == 1:
+                next_prod()
+            if not by_vector:
+                finish(k - 1, 0, False)
+                finish(k - 1, 1, False)
+            m = k + 4
+            if m < 2 * N_PAIRS:
+                if order[m // 2] >= N_Q_PAIRS and m % 2 == 1:
+                    more_loads()
+                bt(m, True)
             if k + 1 < N_UNITS:
-                rp(k + 1)
-            ot_sq(k)
+                rp(k + 1, 2 if k + 1 == N_UNITS - 1 else 1)
+            if by_vector:
+                finish(k - 1, 0, True)
+                finish(k - 1, 1, True)
+            where = "tp" if (k >= N_UNITS - 4 and k % 2 == 1) else "ot"
+            if k < N_UNITS - 1:
+                ot(k, 0, where)
+                ot(k, 1, where)
+                sq(k, 0)
+                rs(k, 0)
+                sq(k, 1)
+                rs(k, 1)
+            else:
+                for b2 in range(2):
+                    ot(k, b2, where)
+                    sq(k, b2)
+                    rs(k, b2)
+                    finish(k, b2, True)
             flush_late()
-            n, e = divmod(k + 3, 2)
-            if e == 0 and n < N_PAIRS:
-                qw(n)
-        finish(N_UNITS - 1, True)
+            if (k + 3) % 2 == 0 and (k + 3) // 2 < N_PAIRS:
+                qw((k + 3) // 2)

@@ -160,7 +160,7 @@ def tile_gqaselfattention_pa_kernel(
 
         def xt_(i, where):
             h, tl = divmod(i, 4)
-            transpose_rows(x_sb[i][:], xg[h][:].bitcast(F32)[:, :, tl * P : (tl + 1) * P, :], False, where, True)
+            transpose_rows(x_sb[i][:], xg[h][:].bitcast(F32)[:, :, tl * P : (tl + 1) * P, :], False, where, False)
 
         def qx(h, tp2):
             for g in range(PASSES):
@@ -249,6 +249,23 @@ def tile_gqaselfattention_pa_kernel(
                     )
             acc_of[u] = acc
 
+        def rp_shared(u):
+            j = order[u // 2]
+            acc = acc_of[u]
+            prods = []
+            for i in range(4):
+                t = tpool.tile([P, HALF], F32, name="t%d" % i, tag="t%d" % i)
+                prods.append(t)
+            odd = tpool.tile([P, HALF], F32, name="odd", tag="odd")
+            nc.scalar.activation(out=odd[:], in_=acc[1][:], func=ACT.Identity, bias=bias_sb[:, 1, j : j + 1], scale=1.0)
+            for i, tab in ((0, ctab_f), (2, stab_f)):
+                nc.vector.scalar_tensor_tensor(
+                    out=prods[i][:], in0=acc[0][:], scalar=bias_sb[:, 0, j : j + 1], in1=tab, op0=ALU.add, op1=ALU.mult
+                )
+            for i, tab in ((1, ntab_f), (3, ctab_f)):
+                nc.gpsimd.tensor_tensor(out=prods[i][:], in0=odd[:], in1=tab, op=ALU.mult)
+            prods_of[u] = prods
+
         def rp(u, pieces=1):
             j = order[u // 2]
             acc = acc_of[u]
@@ -303,13 +320,19 @@ def tile_gqaselfattention_pa_kernel(
                 func=ACT.Abs_reciprocal_sqrt, bias=EPS, scale=1.0 / 128.0,
             )
 
+        def rs_unit(u):
+            nc.scalar.activation(
+                out=rstd_of[u][:].rearrange("p (b c) -> p b c", b=2)[:, :, 0:4],
+                in_=ss_of[u][:].rearrange("p (b c) -> p b c", b=2)[:, :, 0:4],
+                func=ACT.Abs_reciprocal_sqrt, bias=EPS, scale=1.0 / 128.0,
+            )
+
         def ot_sq(u):
             ot(u, 0)
             ot(u, 1)
             sq(u, 0)
-            rs(u, 0)
             sq(u, 1)
-            rs(u, 1)
+            rs_unit(u)
 
         def finish(u, b2, on_vector):
             n, h = divmod(u, 2)
@@ -400,23 +423,23 @@ def tile_gqaselfattention_pa_kernel(
         bt(1, False, ("mx", "mx"))
         xt_(3, ("mx", "mx"))
         next_prod(1)
-        qx(0, 1)
         qw(0)
+        qx(0, 1)
         xt_(4, ("tp", "ot"))
         xt_(5, ("tp", "ot"))
         mx(0)
+        next_prod(1)
+        bt(2, False, ("tp", "ot"))
         qx(1, 0)
         xt_(6, ("tp", "ot"))
         xt_(7, ("tp", "ot"))
-        next_prod(1)
-        qx(1, 1)
-        rp(0)
-        mx(1)
-        bt(2, False, ("tp", "ot"))
         bt(3, False, ("tp", "ot"))
+        rp(0)
+        qx(1, 1)
+        mx(1)
         setup_gains()
-        next_prod(1)
         qw(1)
+        next_prod(1)
         rp(1)
         ot_sq(0)
         bt(4, False)
@@ -434,9 +457,12 @@ def tile_gqaselfattention_pa_kernel(
             if m < 2 * N_PAIRS:
                 if order[m // 2] >= N_Q_PAIRS and m % 2 == 1:
                     more_loads()
-                bt(m, True)
+                bt(m, False)
             if k + 1 < N_UNITS:
-                rp(k + 1, 2 if k + 1 == N_UNITS - 1 else 1)
+                if False:
+                    rp_shared(k + 1)
+                else:
+                    rp(k + 1, 2 if k + 1 == N_UNITS - 1 else 1)
             if by_vector:
                 finish(k - 1, 0, True)
                 finish(k - 1, 1, True)
@@ -445,9 +471,8 @@ def tile_gqaselfattention_pa_kernel(
                 ot(k, 0, where)
                 ot(k, 1, where)
                 sq(k, 0)
-                rs(k, 0)
                 sq(k, 1)
-                rs(k, 1)
+                rs_unit(k)
             else:
                 for b2 in range(2):
                     ot(k, b2, where)

@@ -22,7 +22,6 @@ N_Q_PAIRS = 8
 N_K_PAIRS = 2
 N_PAIRS = N_Q_PAIRS + N_K_PAIRS
 N_UNITS = 2 * N_PAIRS
-N_WARM = 6
 V_TAIL = 2
 
 FLOPS = 2 * TOKENS * (2048 + 512) * K
@@ -62,8 +61,6 @@ def tile_gqaselfattention_pa_kernel(
         sc_bc = const.tile([P, K], F32, name="sc_bc")
         wq_bc = const.tile([P, P], BF16, name="wq_bc")
         wk_bc = const.tile([P, P], BF16, name="wk_bc")
-        zeros = const.tile([P, HALF], BF16, name="zeros")
-        nc.vector.memset(zeros[:], 0.0)
         nc.vector.memset(brow_bf[:], 0.0)
         nc.vector.memset(warm[:], 1.0)
         make_identity(nc, ident[:])
@@ -81,12 +78,8 @@ def tile_gqaselfattention_pa_kernel(
 
         ctx.enter_context(tc.manual_schedule())
 
-        nc.scalar.dma_start(out=cs_bf[:, 0, :, :], in_=cos.rearrange("(b p) i -> p b i", p=P))
-        nc.scalar.dma_start(out=cs_bf[:, 1, :, :], in_=sin.rearrange("(b p) i -> p b i", p=P))
-        nc.scalar.dma_start(out=brow_bf[0:N_Q_PAIRS, :], in_=bq.rearrange("(j c) -> j c", c=256))
-        nc.scalar.dma_start(
-            out=brow_bf[N_Q_PAIRS : N_Q_PAIRS + N_K_PAIRS, :], in_=bk.rearrange("(j c) -> j c", c=256)
-        )
+        nc.sync.dma_start(out=cs_bf[:, 0, :, :], in_=cos.rearrange("(b p) i -> p b i", p=P))
+        nc.sync.dma_start(out=cs_bf[:, 1, :, :], in_=sin.rearrange("(b p) i -> p b i", p=P))
         nc.scalar.activation(out=warm_out[:], in_=warm[:], func=ACT.Abs_reciprocal_sqrt)
 
         wb_of = {}
@@ -115,23 +108,18 @@ def tile_gqaselfattention_pa_kernel(
                 by_of[n] = by
                 nc.sync.dma_start(out=by[:], in_=wq_view[j])
 
-        def prod(n, e):
-            if e == 0:
+        def prod(n, e, lo=0, hi=K):
+            if n not in wb_of:
                 wb = wbpool.tile([P, 2, K], BF16, name="wb", tag="wb")
                 wb_of[n] = wb
             nc.vector.tensor_tensor(
-                out=wb_of[n][:, e, :], in0=by_of[n][:, e, :].bitcast(FP8), in1=sc_bc[:], op=ALU.mult
+                out=wb_of[n][:, e, lo:hi], in0=by_of[n][:, e, lo:hi].bitcast(FP8), in1=sc_bc[:, lo:hi], op=ALU.mult
             )
 
         def flush_late():
             for tp, dst in late:
                 nc.scalar.copy(out=dst, in_=tp[:].rearrange("p g u r -> p g r u"))
             late.clear()
-
-        def dummy(bank):
-            nc.tensor.matmul(
-                out=bank[:].rearrange("p a b c -> p (a b c)"), lhsT=zeros[:, 0:P], rhs=zeros[:], start=True, stop=True
-            )
 
         def head_bank(where):
             if where == "mx":
@@ -142,12 +130,10 @@ def tile_gqaselfattention_pa_kernel(
                 bank = ps_tp.tile([P, 2, 2, P], F32, name="tp", tag="tp")
             return bank
 
-        def transpose_rows(src_bf, dst_words, defer, where=("tp", "tp"), warm_first=False):
+        def transpose_rows(src_bf, dst_words, defer, where=("tp", "tp")):
             words = src_bf.bitcast(F32)
             for gp in range(2):
                 tp = head_bank(where[gp])
-                if warm_first and gp == 0:
-                    dummy(tp)
                 for g2 in range(2):
                     g = 2 * gp + g2
                     for u in range(2):
@@ -160,7 +146,7 @@ def tile_gqaselfattention_pa_kernel(
 
         def xt_(i, where):
             h, tl = divmod(i, 4)
-            transpose_rows(x_sb[i][:], xg[h][:].bitcast(F32)[:, :, tl * P : (tl + 1) * P, :], False, where, False)
+            transpose_rows(x_sb[i][:], xg[h][:].bitcast(F32)[:, :, tl * P : (tl + 1) * P, :], False, where)
 
         def qx(h, tp2):
             for g in range(PASSES):
@@ -171,12 +157,12 @@ def tile_gqaselfattention_pa_kernel(
                     in_=xg[h][:, g, tp2 * 256 : (tp2 + 1) * 256, :].rearrange("p n t -> p (n t)"),
                 )
 
-        def bt(m, defer, where=("tp", "tp"), warm_first=False):
+        def bt(m, defer, where=("tp", "tp")):
             n, e = divmod(m, 2)
             if e == 0:
                 wg = gpool.tile([P, 2, PASSES, P, 4], BF16, name="wg", tag="wg", align_bytes=64)
                 wg_of[n] = wg
-            transpose_rows(wb_of[n][:, e, :], wg_of[n][:].bitcast(F32)[:, e, :, :, :], defer, where, warm_first)
+            transpose_rows(wb_of[n][:, e, :], wg_of[n][:].bitcast(F32)[:, e, :, :, :], defer, where)
 
         def qw(n):
             wc = wpool.tile([P, 2 * PASSES * P], U32, name="wc", tag="wc", align_bytes=64)
@@ -191,8 +177,7 @@ def tile_gqaselfattention_pa_kernel(
 
         def setup_widen():
             for hh in range(2):
-                nc.vector.tensor_copy(out=cs_f[:, :, :, hh, :], in_=cs_bf[:])
-            nc.vector.tensor_copy(out=brow_f[:], in_=brow_bf[:])
+                nc.scalar.copy(out=cs_f[:, :, :, hh, :], in_=cs_bf[:])
 
         def setup_tables():
             tp_cs = ps_ot.tile([P, 2, 2, P], F32, name="ot", tag="ot")
@@ -202,16 +187,17 @@ def tile_gqaselfattention_pa_kernel(
                         tp_cs[:, c, b, :], cs_f[:, c, b, :, :].rearrange("p h i -> p (h i)"), ident[:]
                     )
             for rep in range(2):
-                nc.vector.tensor_copy(out=ctab[:, rep, :], in_=tp_cs[:, 0, :, :].rearrange("p b t -> p (b t)"))
-                nc.vector.tensor_copy(out=stab[:, rep, :], in_=tp_cs[:, 1, :, :].rearrange("p b t -> p (b t)"))
-                nc.vector.tensor_scalar_mul(
-                    out=ntab[:, rep, :], in0=tp_cs[:, 1, :, :].rearrange("p b t -> p (b t)"), scalar1=-1.0
-                )
+                nc.scalar.copy(out=ctab[:, rep, :], in_=tp_cs[:, 0, :, :].rearrange("p b t -> p (b t)"))
+                nc.scalar.copy(out=stab[:, rep, :], in_=tp_cs[:, 1, :, :].rearrange("p b t -> p (b t)"))
+                nc.scalar.mul(out=ntab[:, rep, :], in_=tp_cs[:, 1, :, :].rearrange("p b t -> p (b t)"), mul=-1.0)
+
+        def setup_bias():
+            nc.scalar.copy(out=brow_f[:], in_=brow_bf[:])
             tp_b = ps_ot.tile([P, 2, 2, P], F32, name="ot", tag="ot")
             brow_v = brow_f[:].rearrange("p (c e) -> p e c", e=2)
             for e in range(2):
                 nc.tensor.transpose(tp_b[:, 0, e, :], brow_v[:, e, :], ident[:])
-            nc.vector.tensor_copy(out=bias_sb[:, :, 0:10], in_=tp_b[:, 0, :, 0:10])
+            nc.scalar.copy(out=bias_sb[:, :, 0:10], in_=tp_b[:, 0, :, 0:10])
 
         def setup_gains():
             for wr, src in ((w_rep_q, wq_bc), (w_rep_k, wk_bc)):
@@ -381,8 +367,17 @@ def tile_gqaselfattention_pa_kernel(
                 in_=y[:, 2 * b2 : 2 * b2 + 2, :, :].rearrange("p b h d -> p b (h d)"),
             )
 
-        nc.sync.dma_start(out=sc_bc[:], in_=Wq_scale.rearrange("o k -> (o k)").partition_broadcast(P))
-        for kind, i in (("w", 0), ("x", 0), ("x", 1), ("x", 2), ("x", 3), ("w", 1), ("x", 4), ("x", 5), ("x", 6), ("x", 7), ("w", 2), ("w", 3), ("w", 4)):
+        load_w(0)
+        for c in range(2):
+            nc.sync.dma_start(
+                out=sc_bc[:, c * 1024 : (c + 1) * 1024],
+                in_=Wq_scale.rearrange("o k -> (o k)")[c * 1024 : (c + 1) * 1024].partition_broadcast(P),
+            )
+        nc.sync.dma_start(out=brow_bf[0:N_Q_PAIRS, :], in_=bq.rearrange("(j c) -> j c", c=256))
+        nc.sync.dma_start(
+            out=brow_bf[N_Q_PAIRS : N_Q_PAIRS + N_K_PAIRS, :], in_=bk.rearrange("(j c) -> j c", c=256)
+        )
+        for kind, i in (("x", 0), ("x", 1), ("x", 2), ("x", 3), ("w", 1), ("x", 4), ("x", 5), ("x", 6), ("x", 7), ("w", 2), ("w", 3), ("w", 4)):
             if kind == "x":
                 load_x(i)
             else:
@@ -410,11 +405,13 @@ def tile_gqaselfattention_pa_kernel(
             return state["p"] < len(qhalves) and qhalves[state["p"]] <= k + 5
 
         setup_widen()
-        first = head_bank("mx")
-        for i in range(N_WARM):
-            dummy(first)
         setup_tables()
-        next_prod(2)
+        setup_bias()
+        for c in range(2):
+            for e in range(2):
+                prod(0, e, c * 1024, (c + 1) * 1024)
+        state["p"] = 2
+        more_loads()
         xt_(0, ("mx", "mx"))
         xt_(1, ("mx", "mx"))
         qx(0, 0)

from contextlib import ExitStack

import concourse.mybir as mybir
from concourse.masks import make_identity

F32 = mybir.dt.float32
BF16 = mybir.dt.bfloat16
U32 = mybir.dt.uint32
U8 = mybir.dt.uint8
FP8 = mybir.dt.float8_e4m3fn
FP8X4 = mybir.dt.float8_e4m3fn_x4
ALU = mybir.AluOpType
ACT = mybir.ActivationFunctionType

P = 128
K = 2048
PASSES = 4
TOKENS = 1024
HALF = 512
EPS = 1e-6
N_Q_PAIRS = 8
N_K_PAIRS = 2
N_PAIRS = N_Q_PAIRS + N_K_PAIRS
N_UNITS = 2 * N_PAIRS
V_TAIL = 2

FLOPS = 2 * TOKENS * (2048 + 512) * K


def tile_gqaselfattention_pa_kernel(
    tc, x, Wq_bytes, Wq_scale, bq, Wk, bk, qn_w, kn_w, cos, sin, out_0, out_1
):
    nc = tc.nc
    x_view = x.flatten_outer_dims().rearrange("(n p) k -> n p k", p=P)
    wq_view = Wq_bytes.rearrange("(j p e) k -> j p e k", p=P, e=2)
    wk_view = Wk.rearrange("(j p e) k -> j p e k", p=P, e=2)
    oq_view = out_0.rearrange("b t h d -> (b t) (h d)").rearrange("(n p) c -> p n c", p=P)
    ok_view = out_1.rearrange("b t h d -> (b t) (h d)").rearrange("(n p) c -> p n c", p=P)
    order = [0, 1, 8, 2, 3, 4, 9, 5, 6, 7]

    with ExitStack() as ctx:
        const = ctx.enter_context(tc.tile_pool(name="const", bufs=1))
        xin = ctx.enter_context(tc.tile_pool(name="xin", bufs=8))
        xkeep = ctx.enter_context(tc.tile_pool(name="xkeep", bufs=1))
        bpool = ctx.enter_context(tc.tile_pool(name="bpool", bufs=4))
        wbpool = ctx.enter_context(tc.tile_pool(name="wbpool", bufs=5))
        wpool = ctx.enter_context(tc.tile_pool(name="wpool", bufs=3))
        gpool = ctx.enter_context(tc.tile_pool(name="gpool", bufs=2))
        tpool = ctx.enter_context(tc.tile_pool(name="tpool", bufs=2))
        ypool = ctx.enter_context(tc.tile_pool(name="ypool", bufs=3))
        spool = ctx.enter_context(tc.tile_pool(name="spool", bufs=4))
        ps_tp = ctx.enter_context(tc.psum_pool(name="ps_tp", bufs=2))
        ps_mx = ctx.enter_context(tc.psum_pool(name="ps_mx", bufs=4))
        ps_ot = ctx.enter_context(tc.psum_pool(name="ps_ot", bufs=2))

        cs_bf = const.tile([P, 2, 2, 64], BF16, name="cs_bf")
        brow_bf = const.tile([P, 256], BF16, name="brow_bf")
        warm = const.tile([P, 1], F32, name="warm")
        warm_out = const.tile([P, 1], F32, name="warm_out")
        ident = const.tile([P, P], F32, name="ident")
        sc_bc = const.tile([P, K], F32, name="sc_bc")
        wq_bc = const.tile([P, P], BF16, name="wq_bc")
        wk_bc = const.tile([P, P], BF16, name="wk_bc")
        nc.vector.memset(brow_bf[:], 0.0)
        nc.vector.memset(warm[:], 1.0)
        make_identity(nc, ident[:])

        x_sb = []
        for n in range(8):
            xt = xin.tile([P, K], BF16, name="x_sb", tag="x_sb")
            x_sb.append(xt)
        xc = xkeep.tile([P, PASSES, TOKENS], U32, name="xc", align_bytes=64)
        xs = xkeep.tile([P, PASSES, TOKENS], U8, name="xs", align_bytes=64)
        xg = []
        for h in range(2):
            xgh = xkeep.tile([P, PASSES, HALF, 4], BF16, name="xg%d" % h, align_bytes=64)
            xg.append(xgh)

        ctx.enter_context(tc.manual_schedule())

        nc.sync.dma_start(out=cs_bf[:, 0, :, :], in_=cos.rearrange("(b p) i -> p b i", p=P))
        nc.sync.dma_start(out=cs_bf[:, 1, :, :], in_=sin.rearrange("(b p) i -> p b i", p=P))
        nc.scalar.activation(out=warm_out[:], in_=warm[:], func=ACT.Abs_reciprocal_sqrt)

        wb_of = {}
        by_of = {}
        wg_of = {}
        codes_of = {}
        acc_of = {}
        prods_of = {}
        ots_of = {}
        ss_of = {}
        rstd_of = {}
        y_of = {}
        late = []

        def load_x(i):
            nc.sync.dma_start(out=x_sb[i][:], in_=x_view[i])

        def load_w(n):
            j = order[n]
            if j >= N_Q_PAIRS:
                wb = wbpool.tile([P, 2, K], BF16, name="wb", tag="wb")
                wb_of[n] = wb
                nc.sync.dma_start(out=wb[:], in_=wk_view[j - N_Q_PAIRS])
            else:
                by = bpool.tile([P, 2, K], U8, name="wq_bytes_sb", tag="wq_bytes_sb")
                by_of[n] = by
                nc.sync.dma_start(out=by[:], in_=wq_view[j])

        def prod(n, e, lo=0, hi=K):
            if n not in wb_of:
                wb = wbpool.tile([P, 2, K], BF16, name="wb", tag="wb")
                wb_of[n] = wb
            nc.vector.tensor_tensor(
                out=wb_of[n][:, e, lo:hi], in0=by_of[n][:, e, lo:hi].bitcast(FP8), in1=sc_bc[:, lo:hi], op=ALU.mult
            )

        def flush_late():
            for tp, dst in late:
                nc.scalar.copy(out=dst, in_=tp[:].rearrange("p g u r -> p g r u"))
            late.clear()

        def head_bank(where):
            if where == "mx":
                bank = ps_mx.tile([P, 2, 2, P], F32, name="mx", tag="mx")
            elif where == "ot":
                bank = ps_ot.tile([P, 2, 2, P], F32, name="ot", tag="ot")
            else:
                bank = ps_tp.tile([P, 2, 2, P], F32, name="tp", tag="tp")
            return bank

        def transpose_rows(src_bf, dst_words, defer, where=("tp", "tp")):
            words = src_bf.bitcast(F32)
            for gp in range(2):
                tp = head_bank(where[gp])
                for g2 in range(2):
                    g = 2 * gp + g2
                    for u in range(2):
                        nc.tensor.transpose(
                            tp[:, g2, u, :], words[:, 256 * g + u : 256 * (g + 1) : 2], ident[:]
                        )
                late.append((tp, dst_words[:, 2 * gp : 2 * gp + 2, :, :]))
                if not (defer and gp == 1):
                    flush_late()

        def xt_(i, where):
            h, tl = divmod(i, 4)
            transpose_rows(x_sb[i][:], xg[h][:].bitcast(F32)[:, :, tl * P : (tl + 1) * P, :], False, where)

        def qx(h, tp2):
            for g in range(PASSES):
                lo = h * HALF + tp2 * 256
                nc.vector.quantize_mx(
                    out=xc[:, g, lo : lo + 256].bitcast(FP8X4),
                    scales=xs[:, g, lo : lo + 256],
                    in_=xg[h][:, g, tp2 * 256 : (tp2 + 1) * 256, :].rearrange("p n t -> p (n t)"),
                )

        def bt(m, defer, where=("tp", "tp")):
            n, e = divmod(m, 2)
            if e == 0:
                wg = gpool.tile([P, 2, PASSES, P, 4], BF16, name="wg", tag="wg", align_bytes=64)
                wg_of[n] = wg
            transpose_rows(wb_of[n][:, e, :], wg_of[n][:].bitcast(F32)[:, e, :, :, :], defer, where)

        def qw(n):
            wc = wpool.tile([P, 2 * PASSES * P], U32, name="wc", tag="wc", align_bytes=64)
            ws = wpool.tile([P, 2 * PASSES * P], U8, name="ws", tag="ws", align_bytes=64)
            nc.vector.quantize_mx(
                out=wc[:].bitcast(FP8X4), scales=ws[:], in_=wg_of[n][:].rearrange("p e g r t -> p (e g r t)")
            )
            codes_of[n] = (wc, ws)

        cs_f = const.tile([P, 2, 2, 2, 64], F32, name="cs_f")
        brow_f = const.tile([P, 256], F32, name="brow_f")

        def setup_widen():
            for hh in range(2):
                nc.scalar.copy(out=cs_f[:, :, :, hh, :], in_=cs_bf[:])

        def setup_tables():
            tp_cs = ps_ot.tile([P, 2, 2, P], F32, name="ot", tag="ot")
            for c in range(2):
                for b in range(2):
                    nc.tensor.transpose(
                        tp_cs[:, c, b, :], cs_f[:, c, b, :, :].rearrange("p h i -> p (h i)"), ident[:]
                    )
            for rep in range(2):
                nc.scalar.copy(out=ctab[:, rep, :], in_=tp_cs[:, 0, :, :].rearrange("p b t -> p (b t)"))
                nc.scalar.copy(out=stab[:, rep, :], in_=tp_cs[:, 1, :, :].rearrange("p b t -> p (b t)"))
                nc.scalar.mul(out=ntab[:, rep, :], in_=tp_cs[:, 1, :, :].rearrange("p b t -> p (b t)"), mul=-1.0)

        def setup_bias():
            nc.scalar.copy(out=brow_f[:], in_=brow_bf[:])
            tp_b = ps_ot.tile([P, 2, 2, P], F32, name="ot", tag="ot")
            brow_v = brow_f[:].rearrange("p (c e) -> p e c", e=2)
            for e in range(2):
                nc.tensor.transpose(tp_b[:, 0, e, :], brow_v[:, e, :], ident[:])
            nc.scalar.copy(out=bias_sb[:, :, 0:10], in_=tp_b[:, 0, :, 0:10])

        def setup_gains():
            for wr, src in ((w_rep_q, wq_bc), (w_rep_k, wk_bc)):
                for r in range(4):
                    nc.gpsimd.tensor_copy(out=wr[:, r, :], in_=src[:])

        ctab = const.tile([P, 2, 256], F32, name="ctab")
        stab = const.tile([P, 2, 256], F32, name="stab")
        ntab = const.tile([P, 2, 256], F32, name="ntab")
        bias_sb = const.tile([P, 2, 16], F32, name="bias_sb")
        w_rep_q = const.tile([P, 4, P], F32, name="w_rep_q")
        w_rep_k = const.tile([P, 4, P], F32, name="w_rep_k")
        ctab_f = ctab[:].rearrange("p r t -> p (r t)")
        stab_f = stab[:].rearrange("p r t -> p (r t)")
        ntab_f = ntab[:].rearrange("p r t -> p (r t)")

        def mx(u):
            n, h = divmod(u, 2)
            wc, ws = codes_of[n]
            tok = slice(h * HALF, (h + 1) * HALF)
            acc = []
            for e in range(2):
                pe = ps_mx.tile([P, HALF], F32, name="mx", tag="mx")
                acc.append(pe)
                for g in range(PASSES):
                    c = e * PASSES + g
                    nc.tensor.matmul_mx(
                        out=pe[:],
                        lhsT=wc[:, c * P : (c + 1) * P].bitcast(FP8X4),
                        lhsT_scale=ws[:, c * P : (c + 1) * P],
                        rhs=xc[:, g, tok].bitcast(FP8X4),
                        rhs_scale=xs[:, g, tok],
                        start=(g == 0),
                        stop=(g == PASSES - 1),
                    )
            acc_of[u] = acc

        def rp_shared(u):
            j = order[u // 2]
            acc = acc_of[u]
            prods = []
            for i in range(4):
                t = tpool.tile([P, HALF], F32, name="t%d" % i, tag="t%d" % i)
                prods.append(t)
            odd = tpool.tile([P, HALF], F32, name="odd", tag="odd")
            nc.scalar.activation(out=odd[:], in_=acc[1][:], func=ACT.Identity, bias=bias_sb[:, 1, j : j + 1], scale=1.0)
            for i, tab in ((0, ctab_f), (2, stab_f)):
                nc.vector.scalar_tensor_tensor(
                    out=prods[i][:], in0=acc[0][:], scalar=bias_sb[:, 0, j : j + 1], in1=tab, op0=ALU.add, op1=ALU.mult
                )
            for i, tab in ((1, ntab_f), (3, ctab_f)):
                nc.gpsimd.tensor_tensor(out=prods[i][:], in0=odd[:], in1=tab, op=ALU.mult)
            prods_of[u] = prods

        def rp(u, pieces=1):
            j = order[u // 2]
            acc = acc_of[u]
            prods = []
            for i in range(4):
                t = tpool.tile([P, HALF], F32, name="t%d" % i, tag="t%d" % i)
                prods.append(t)
            width = HALF // pieces
            for c in range(pieces):
                cols = slice(c * width, (c + 1) * width)
                for i, (e, tab) in enumerate(((0, ctab_f), (1, ntab_f), (0, stab_f), (1, ctab_f))):
                    nc.vector.scalar_tensor_tensor(
                        out=prods[i][:, cols], in0=acc[e][:, cols], scalar=bias_sb[:, e, j : j + 1], in1=tab[:, cols],
                        op0=ALU.add, op1=ALU.mult,
                    )
            prods_of[u] = prods

        def ot(u, b2, where="ot"):
            prods = prods_of[u]
            bank = head_bank(where)
            ots_of.setdefault(u, []).append(bank)
            for bb in range(2):
                cols = slice((2 * b2 + bb) * P, (2 * b2 + bb + 1) * P)
                for half in range(2):
                    nc.tensor.matmul(
                        out=bank[:, bb, half, :], lhsT=prods[2 * half][:, cols], rhs=ident[:],
                        start=True, stop=False, is_transpose=True,
                    )
                    nc.tensor.matmul(
                        out=bank[:, bb, half, :], lhsT=prods[2 * half + 1][:, cols], rhs=ident[:],
                        start=False, stop=True, is_transpose=True,
                    )

        def sq(u, b2):
            if b2 == 0:
                ss = spool.tile([P, 16], F32, name="ss", tag="ss")
                ss_of[u] = ss
                rstd = spool.tile([P, 16], F32, name="rstd", tag="rstd")
                rstd_of[u] = rstd
            for bb in range(2):
                for hh in range(2):
                    col = 8 * b2 + 2 * bb + hh
                    junk = spool.tile([P, 2, 64], F32, name="junk", tag="junk")
                    nc.scalar.activation(
                        out=junk[:], in_=ots_of[u][b2][:, bb, :, hh * 64 : (hh + 1) * 64], func=ACT.Square,
                        accum_out=ss_of[u][:, col : col + 1],
                    )

        def rs(u, b2):
            nc.scalar.activation(
                out=rstd_of[u][:, 8 * b2 : 8 * b2 + 4], in_=ss_of[u][:, 8 * b2 : 8 * b2 + 4],
                func=ACT.Abs_reciprocal_sqrt, bias=EPS, scale=1.0 / 128.0,
            )

        def rs_unit(u):
            nc.scalar.activation(
                out=rstd_of[u][:].rearrange("p (b c) -> p b c", b=2)[:, :, 0:4],
                in_=ss_of[u][:].rearrange("p (b c) -> p b c", b=2)[:, :, 0:4],
                func=ACT.Abs_reciprocal_sqrt, bias=EPS, scale=1.0 / 128.0,
            )

        def ot_sq(u):
            ot(u, 0)
            ot(u, 1)
            sq(u, 0)
            sq(u, 1)
            rs_unit(u)

        def finish(u, b2, on_vector):
            n, h = divmod(u, 2)
            j = order[n]
            bank = ots_of[u][b2]
            rstd = rstd_of[u]
            wr = w_rep_q if j < N_Q_PAIRS else w_rep_k
            if j < N_Q_PAIRS:
                dst = oq_view[:, 4 * h : 4 * h + 4, 256 * j : 256 * (j + 1)]
            else:
                dst = ok_view[:, 4 * h : 4 * h + 4, 256 * (j - N_Q_PAIRS) : 256 * (j - N_Q_PAIRS + 1)]
            if b2 == 0:
                y = ypool.tile([P, 4, 2, P], F32, name="y", tag="y")
                y_of[u] = y
            y = y_of[u]
            yf = y[:].rearrange("p b h d -> p (b h d)")
            for bb in range(2):
                for hh in range(2):
                    blk = 2 * b2 + bb
                    col = 8 * b2 + 2 * bb + hh
                    if on_vector:
                        nc.vector.scalar_tensor_tensor(
                            out=y[:, blk, hh, :].rearrange("p (a i) -> p a i", a=2),
                            in0=bank[:, bb, :, hh * 64 : (hh + 1) * 64],
                            scalar=rstd[:, col : col + 1],
                            in1=wr[:, 0, :].rearrange("p (a i) -> p a i", a=2),
                            op0=ALU.mult,
                            op1=ALU.mult,
                        )
                    else:
                        nc.scalar.activation(
                            out=y[:, blk, hh, :].rearrange("p (a i) -> p a i", a=2),
                            in_=bank[:, bb, :, hh * 64 : (hh + 1) * 64],
                            func=ACT.Copy,
                            scale=rstd[:, col : col + 1],
                        )
            if not on_vector:
                nc.gpsimd.tensor_tensor(
                    out=yf[:, b2 * 512 : (b2 + 1) * 512],
                    in0=yf[:, b2 * 512 : (b2 + 1) * 512],
                    in1=wr[:].rearrange("p r d -> p (r d)"),
                    op=ALU.mult,
                )
            nc.sync.dma_start(
                out=dst[:, 2 * b2 : 2 * b2 + 2, :],
                in_=y[:, 2 * b2 : 2 * b2 + 2, :, :].rearrange("p b h d -> p b (h d)"),
            )

        load_w(0)
        for c in range(2):
            nc.sync.dma_start(
                out=sc_bc[:, c * 1024 : (c + 1) * 1024],
                in_=Wq_scale.rearrange("o k -> (o k)")[c * 1024 : (c + 1) * 1024].partition_broadcast(P),
            )
        nc.sync.dma_start(out=brow_bf[0:N_Q_PAIRS, :], in_=bq.rearrange("(j c) -> j c", c=256))
        nc.sync.dma_start(
            out=brow_bf[N_Q_PAIRS : N_Q_PAIRS + N_K_PAIRS, :], in_=bk.rearrange("(j c) -> j c", c=256)
        )
        for kind, i in (("x", 0), ("x", 1), ("x", 2), ("x", 3), ("w", 1), ("x", 4), ("x", 5), ("x", 6), ("x", 7), ("w", 2), ("w", 3), ("w", 4)):
            if kind == "x":
                load_x(i)
            else:
                load_w(i)
        nc.sync.dma_start(out=wq_bc[:], in_=qn_w.partition_broadcast(P))
        nc.sync.dma_start(out=wk_bc[:], in_=kn_w.partition_broadcast(P))
        state = {"p": 0, "l": 5}
        qhalves = [2 * n + e for n in range(N_PAIRS) for e in range(2) if order[n] < N_Q_PAIRS]

        def more_loads():
            if state["l"] < N_PAIRS:
                load_w(state["l"])
                state["l"] += 1

        def next_prod(c=1):
            for i in range(c):
                if state["p"] < len(qhalves):
                    n, e = divmod(qhalves[state["p"]], 2)
                    prod(n, e)
                    state["p"] += 1
                    if e == 1:
                        more_loads()

        def due(k):
            return state["p"] < len(qhalves) and qhalves[state["p"]] <= k + 5

        setup_widen()
        setup_tables()
        setup_bias()
        for c in range(2):
            for e in range(2):
                prod(0, e, c * 1024, (c + 1) * 1024)
        state["p"] = 2
        more_loads()
        xt_(0, ("mx", "mx"))
        xt_(1, ("mx", "mx"))
        qx(0, 0)
        bt(0, False, ("mx", "mx"))
        xt_(2, ("mx", "mx"))
        bt(1, False, ("mx", "mx"))
        xt_(3, ("mx", "mx"))
        next_prod(1)
        qw(0)
        qx(0, 1)
        xt_(4, ("tp", "ot"))
        xt_(5, ("tp", "ot"))
        mx(0)
        next_prod(1)
        bt(2, False, ("tp", "ot"))
        qx(1, 0)
        xt_(6, ("tp", "ot"))
        xt_(7, ("tp", "ot"))
        bt(3, False, ("tp", "ot"))
        rp(0)
        qx(1, 1)
        mx(1)
        setup_gains()
        qw(1)
        next_prod(1)
        rp(1)
        ot_sq(0)
        bt(4, False)

        for k in range(1, N_UNITS):
            by_vector = k - 1 >= N_UNITS - V_TAIL
            if k + 1 < N_UNITS:
                mx(k + 1)
            if due(k) or k % 2 == 1:
                next_prod()
            if not by_vector:
                finish(k - 1, 0, False)
                finish(k - 1, 1, False)
            m = k + 4
            if m < 2 * N_PAIRS:
                if order[m // 2] >= N_Q_PAIRS and m % 2 == 1:
                    more_loads()
                bt(m, False)
            if k + 1 < N_UNITS:
                if False:
                    rp_shared(k + 1)
                else:
                    rp(k + 1, 2 if k + 1 == N_UNITS - 1 else 1)
            if by_vector:
                finish(k - 1, 0, True)
                finish(k - 1, 1, True)
            where = "tp" if (k >= N_UNITS - 4 and k % 2 == 1) else "ot"
            if k < N_UNITS - 1:
                ot(k, 0, where)
                ot(k, 1, where)
                sq(k, 0)
                sq(k, 1)
                rs_unit(k)
            else:
                for b2 in range(2):
                    ot(k, b2, where)
                    sq(k, b2)
                    rs(k, b2)
                    finish(k, b2, True)
            flush_late()
            if (k + 3) % 2 == 0 and (k + 3) // 2 < N_PAIRS:
                qw((k + 3) // 2)
